import numpy as np
import ml_dtypes


def mxq(x, axis, fmt="e4m3"):
    dtype, down = {"e4m3": (ml_dtypes.float8_e4m3fn, 7), "e5m2": (ml_dtypes.float8_e5m2, 14)}[fmt]
    v = np.moveaxis(np.asarray(x, np.float32).astype(ml_dtypes.bfloat16).astype(np.float64), axis, -1)
    blocks = v.reshape(v.shape[:-1] + (-1, 32))
    amax = np.abs(blocks).max(-1, keepdims=True)
    byte = np.maximum(np.where(amax > 0, np.frexp(amax)[1] - 1 + 127, 0) - down, 1)
    scale = np.exp2(byte - 127.0)
    codes = (blocks / scale).astype(np.float32).astype(dtype).astype(np.float64)
    return np.moveaxis((codes * scale).reshape(v.shape), -1, axis)


WIDE = False


def mx_kscale(k):
    if not WIDE:
        return np.ones(k)
    levels = np.array([10, -10, 5, -5, 0])
    a = np.random.permutation(np.resize(levels, k // 512 * 4)).reshape(k // 512, 4)
    idx = np.arange(k)
    return np.exp2(a[idx // 512, idx % 128 // 32])


BF16 = ml_dtypes.bfloat16


def bf(x):
    return np.asarray(x, np.float32).astype(BF16)


def f64(x):
    return np.asarray(x).astype(np.float64)


B, L, D, H, DK = 16, 256, 512, 4, 64
E = H * DK


def tropical_linear(t, w):
    return np.stack([np.max(t[n][:, None, :] + w[None, :, :], axis=-1) for n in range(t.shape[0])])


def split_heads(t):
    return t.reshape(B, L, H, DK).transpose(0, 2, 1, 3).reshape(B * H, L, DK)


def proj(xq, w, lam):
    return np.log1p(np.maximum(xq @ mxq(f64(w), 1, "e4m3").T, 0.0)) - lam


def setup_inputs():
    s = mx_kscale(D)
    return {"x": bf(np.random.standard_normal((B, L, D)) * s),
            "Wq": bf(np.random.standard_normal((E, D)) / np.sqrt(D) / s[None, :]),
            "Wk": bf(np.random.standard_normal((E, D)) / np.sqrt(D) / s[None, :]),
            "Wv": bf(np.random.standard_normal((E, D)) / np.sqrt(D) / s[None, :]),
            "lam": bf(1.0 + 0.1 * np.random.standard_normal((1, 1, E))),
            "Wq_trop": bf(np.random.standard_normal((DK, DK))),
            "Wk_trop": bf(np.random.standard_normal((DK, DK))),
            "Wv_trop": bf(np.random.standard_normal((DK, DK)))}


def reference(x, Wq, Wk, Wv, lam, Wq_trop, Wk_trop, Wv_trop):
    xq = mxq(f64(x), 2, "e4m3")
    lam = f64(lam)
    q = tropical_linear(split_heads(proj(xq, Wq, lam)), f64(Wq_trop))
    k = tropical_linear(split_heads(proj(xq, Wk, lam)), f64(Wk_trop))
    v = tropical_linear(split_heads(proj(xq, Wv, lam)), f64(Wv_trop))
    return q, k, v

@@ -1,0 +1,218 @@
+from contextlib import ExitStack
+
+import concourse.mybir as mybir
+from concourse.masks import make_identity
+
+F32 = mybir.dt.float32
+BF16 = mybir.dt.bfloat16
+U32 = mybir.dt.uint32
+U8 = mybir.dt.uint8
+FP8X4 = mybir.dt.float8_e4m3fn_x4
+ALU = mybir.AluOpType
+ACT = mybir.ActivationFunctionType
+AX = mybir.AxisListType
+
+P = 128
+B, L, D, H, DK = 16, 256, 512, 4, 64
+E = H * DK
+ROWS = B * L
+HALF = DK // 2
+CHUNK = 2048
+TILES = CHUNK // P
+PIECE = 512
+CLAMP = 128.0
+
+FLOPS = 2 * ROWS * D * 3 * E + 2 * 3 * ROWS * H * DK * DK
+
+
+def tile_tropicalattention_pa_t_kernel(
+    tc, x, Wq, Wk, Wv, lam, Wq_trop, Wk_trop, Wv_trop, out_0, out_1, out_2
+):
+    nc = tc.nc
+    weights = [Wq, Wk, Wv]
+    trops = [Wq_trop, Wk_trop, Wv_trop]
+    outs = [out_0, out_1, out_2]
+
+    with ExitStack() as ctx:
+        const = ctx.enter_context(tc.tile_pool(name="const", bufs=1))
+        keep = ctx.enter_context(tc.tile_pool(name="keep", bufs=1))
+        tmp = ctx.enter_context(tc.tile_pool(name="tmp", bufs=3))
+        psum = ctx.enter_context(tc.psum_pool(name="psum", bufs=8))
+
+        ident = const.tile([P, P], F32, name="ident")
+        make_identity(nc, ident[:])
+
+        x_codes = keep.tile([P, ROWS], U32, name="x_codes", align_bytes=64)
+        x_scales = keep.tile([P, ROWS], U8, name="x_scales", align_bytes=64)
+        w_codes = [keep.tile([P, 2 * P], U32, name="w_codes%d" % j, align_bytes=64) for j in range(3)]
+        w_scales = [keep.tile([P, 2 * P], U8, name="w_scales%d" % j, align_bytes=64) for j in range(3)]
+        diff = [keep.tile([P, ROWS], F32, name="diff%d" % j) for j in range(3)]
+        base = [keep.tile([P, ROWS], F32, name="base%d" % j) for j in range(3)]
+        delta = [keep.tile([P, DK], F32, name="delta%d" % j) for j in range(3)]
+        shift = [keep.tile([P, DK], F32, name="shift%d" % j) for j in range(3)]
+
+        with tc.tile_pool(name="stage", bufs=2) as stage, tc.tile_pool(name="small", bufs=1) as small:
+            w_sb = []
+            for j in range(3):
+                w_t = small.tile([P, 2 * D], BF16, name="w_sb%d" % j)
+                nc.sync.dma_start(
+                    out=w_t[:].rearrange("p (g k) -> p g k", g=2),
+                    in_=weights[j].rearrange("(g p) k -> p g k", p=P),
+                )
+                w_sb.append(w_t)
+            lam_b = small.tile([P, E], BF16, name="lam_b")
+            nc.scalar.dma_start(out=lam_b[:], in_=lam.rearrange("a b e -> (a b e)").partition_broadcast(P))
+            t_sb = []
+            for j in range(3):
+                t_t = small.tile([P, DK], BF16, name="t_sb%d" % j)
+                nc.scalar.dma_start(out=t_t[0:DK, :], in_=trops[j])
+                nc.scalar.dma_start(out=t_t[DK:P, :], in_=trops[j])
+                t_sb.append(t_t)
+
+            for j in range(3):
+                words = w_sb[j][:].bitcast(F32)
+                bank = psum.tile([P, 512], F32, name="bank", tag="bank")
+                for g in range(2):
+                    for u in range(2):
+                        nc.tensor.transpose(
+                            bank[:, u * 256 + g * P : u * 256 + (g + 1) * P],
+                            words[:, g * 256 + u * P : g * 256 + (u + 1) * P],
+                            ident[:],
+                        )
+                gw = small.tile([P, 2 * D], BF16, name="gw%d" % j, align_bytes=64)
+                src = bank[:].rearrange("p (u h i l) -> p i h l u", u=2, h=H, i=2, l=HALF)
+                dst = gw[:].bitcast(F32).rearrange("p (i h l u) -> p i h l u", i=2, h=H, l=HALF, u=2)
+                for i in range(2):
+                    nc.vector.tensor_copy(out=dst[:, i], in_=src[:, i])
+                nc.vector.quantize_mx(out=w_codes[j][:].bitcast(FP8X4), scales=w_scales[j][:], in_=gw[:])
+
+            lam_v = lam_b[:].rearrange("p (h i l) -> p h i l", h=H, i=2, l=HALF)
+            for j in range(3):
+                xab = small.tile([P, 2 * P], F32, name="xab%d" % j)
+                for i in range(2):
+                    nc.vector.tensor_tensor(
+                        out=xab[:, i * P : (i + 1) * P].rearrange("p (h l) -> p h l", h=H),
+                        in0=t_sb[j][:, i * HALF : (i + 1) * HALF].unsqueeze(1).to_broadcast([P, H, HALF]),
+                        in1=lam_v[:, :, i, :],
+                        op=ALU.subtract,
+                    )
+                bank = psum.tile([P, 512], F32, name="bank", tag="bank")
+                for i in range(2):
+                    nc.tensor.transpose(bank[:, i * P : (i + 1) * P], xab[:, i * P : (i + 1) * P], ident[:])
+                tab = small.tile([P, 2, DK], F32, name="tab%d" % j)
+                nc.vector.tensor_copy(
+                    out=tab[:], in_=bank[:, 0 : 2 * P].rearrange("p (i o) -> p i o", i=2)[:, :, 0:DK]
+                )
+                nc.vector.tensor_tensor(out=delta[j][:], in0=tab[:, 0, :], in1=tab[:, 1, :], op=ALU.subtract)
+                nc.vector.tensor_scalar(
+                    out=delta[j][:], in0=delta[j][:], scalar1=CLAMP, scalar2=-CLAMP, op0=ALU.min, op1=ALU.max
+                )
+                nc.vector.scalar_tensor_tensor(
+                    out=shift[j][:], in0=tab[:, 0, :], scalar=-CLAMP, in1=tab[:, 1, :], op0=ALU.add, op1=ALU.max
+                )
+
+            x_view = x.flatten_outer_dims().rearrange("(t p) k -> p t k", p=P)
+            for c in range(4):
+                xs = stage.tile([P, 8 * D], BF16, name="xs", tag="xs")
+                nc.sync.dma_start(
+                    out=xs[:].rearrange("p (t k) -> p t k", t=8), in_=x_view[:, 8 * c : 8 * c + 8, :]
+                )
+                words = xs[:].bitcast(F32)
+                gx = stage.tile([P, 8 * D], BF16, name="gx", tag="gx", align_bytes=64)
+                gx_words = gx[:].bitcast(F32)
+                for pr in range(4):
+                    bank = psum.tile([P, 512], F32, name="bank", tag="bank")
+                    for tt in range(2):
+                        for u in range(2):
+                            t = 2 * pr + tt
+                            nc.tensor.transpose(
+                                bank[:, u * 256 + tt * P : u * 256 + (tt + 1) * P],
+                                words[:, t * 256 + u * P : t * 256 + (u + 1) * P],
+                                ident[:],
+                            )
+                    dst = gx_words[:, pr * 512 : (pr + 1) * 512].rearrange("p (r u) -> p r u", u=2)
+                    src = bank[:].rearrange("p (u r) -> p r u", u=2)
+                    if pr % 2 == 0:
+                        nc.vector.tensor_copy(out=dst, in_=src)
+                    else:
+                        nc.scalar.copy(out=dst, in_=src)
+                nc.vector.quantize_mx(
+                    out=x_codes[:, c * 1024 : (c + 1) * 1024].bitcast(FP8X4),
+                    scales=x_scales[:, c * 1024 : (c + 1) * 1024],
+                    in_=gx[:],
+                )
+
+        relu_pool = ctx.enter_context(tc.tile_pool(name="relu_pool", bufs=3))
+        base_pool = ctx.enter_context(tc.tile_pool(name="base_pool", bufs=3))
+        y_pool = ctx.enter_context(tc.tile_pool(name="y_pool", bufs=2))
+
+        def prep_piece(j, c):
+            cols = slice(c * PIECE, (c + 1) * PIECE)
+            for i in range(2):
+                bank = psum.tile([P, 512], F32, name="bank", tag="bank")
+                nc.tensor.matmul_mx(
+                    out=bank[:],
+                    lhsT=w_codes[j][:, i * P : (i + 1) * P].bitcast(FP8X4),
+                    lhsT_scale=w_scales[j][:, i * P : (i + 1) * P],
+                    rhs=x_codes[:, cols].bitcast(FP8X4),
+                    rhs_scale=x_scales[:, cols],
+                    start=True,
+                    stop=True,
+                )
+                one_plus = tmp.tile([P, PIECE], F32, name="one_plus", tag="one_plus")
+                nc.vector.tensor_scalar(
+                    out=one_plus[:], in0=bank[:], scalar1=0.0, scalar2=1.0, op0=ALU.max, op1=ALU.add
+                )
+                target = diff[j] if i == 0 else base[j]
+                nc.scalar.activation(out=target[:, cols], in_=one_plus[:], func=ACT.Ln)
+            nc.vector.tensor_tensor(out=diff[j][:, cols], in0=diff[j][:, cols], in1=base[j][:, cols], op=ALU.subtract)
+
+        pieces = [(j, c) for j in range(3) for c in range(ROWS // PIECE)]
+        for k in range(4):
+            prep_piece(*pieces[k])
+        next_piece = 4
+
+        step = 0
+        for j in range(3):
+            for chunk in range(ROWS // CHUNK):
+                rows = slice(chunk * CHUNK, (chunk + 1) * CHUNK)
+                y = y_pool.tile([P, TILES, H, DK], F32, name="y", tag="y")
+                for o in range(DK):
+                    if step % 16 == 0 and next_piece < len(pieces):
+                        prep_piece(*pieces[next_piece])
+                        next_piece += 1
+                    step += 1
+                    gain = relu_pool.tile([P, CHUNK], F32, name="gain", tag="gain")
+                    nc.scalar.activation(
+                        out=gain[:], in_=diff[j][:, rows], func=ACT.Relu, bias=delta[j][:, o : o + 1], scale=1.0
+                    )
+                    floor = base_pool.tile([P, CHUNK], F32, name="floor", tag="floor")
+                    nc.gpsimd.tensor_scalar(
+                        out=floor[:], in0=base[j][:, rows], scalar1=shift[j][:, o : o + 1], scalar2=1.0,
+                        op0=ALU.add, op1=ALU.mult,
+                    )
+                    for q in range(TILES // 4):
+                        bank = psum.tile([P, 512], F32, name="bank", tag="bank")
+                        for s in range(4):
+                            t = 4 * q + s
+                            nc.tensor.matmul(
+                                out=bank[:, s * P : (s + 1) * P], lhsT=gain[:, t * P : (t + 1) * P], rhs=ident[:],
+                                is_transpose=True, start=True, stop=False,
+                            )
+                            nc.tensor.matmul(
+                                out=bank[:, s * P : (s + 1) * P], lhsT=floor[:, t * P : (t + 1) * P], rhs=ident[:],
+                                is_transpose=True, start=False, stop=True,
+                            )
+                        nc.vector.tensor_reduce(
+                            out=y[:, 4 * q : 4 * q + 4, :, o],
+                            in_=bank[:].rearrange("p (s h l) -> p s h l", s=4, h=H, l=HALF),
+                            axis=AX.X,
+                            op=ALU.max,
+                        )
+                for t in range(TILES):
+                    g = chunk * TILES + t
+                    b, l0 = g // 2, (g % 2) * P
+                    nc.sync.dma_start(
+                        out=outs[j][b * H : (b + 1) * H, l0 : l0 + P, :].rearrange("h p o -> p h o"),
+                        in_=y[:, t, :, :],
+                    )

@@ -21,6 +21,7 @@ CHUNK = 2048
 TILES = CHUNK // P
 PIECE = 512
 CLAMP = 128.0
+MERGED = (1, 2)
 
 FLOPS = 2 * ROWS * D * 3 * E + 2 * 3 * ROWS * H * DK * DK
 
@@ -36,117 +37,134 @@ def tile_tropicalattention_pa_t_kernel(
     with ExitStack() as ctx:
         const = ctx.enter_context(tc.tile_pool(name="const", bufs=1))
         keep = ctx.enter_context(tc.tile_pool(name="keep", bufs=1))
+        small = ctx.enter_context(tc.tile_pool(name="small", bufs=1))
         tmp = ctx.enter_context(tc.tile_pool(name="tmp", bufs=3))
+        relu_pool = ctx.enter_context(tc.tile_pool(name="relu_pool", bufs=3))
+        base_pool = ctx.enter_context(tc.tile_pool(name="base_pool", bufs=3))
+        y_pool = ctx.enter_context(tc.tile_pool(name="y_pool", bufs=2))
         psum = ctx.enter_context(tc.psum_pool(name="psum", bufs=8))
 
         ident = const.tile([P, P], F32, name="ident")
         make_identity(nc, ident[:])
+        ones = const.tile([P, 1], F32, name="ones")
+        nc.vector.memset(ones[:], 1.0)
 
         x_codes = keep.tile([P, ROWS], U32, name="x_codes", align_bytes=64)
         x_scales = keep.tile([P, ROWS], U8, name="x_scales", align_bytes=64)
         w_codes = [keep.tile([P, 2 * P], U32, name="w_codes%d" % j, align_bytes=64) for j in range(3)]
         w_scales = [keep.tile([P, 2 * P], U8, name="w_scales%d" % j, align_bytes=64) for j in range(3)]
-        diff = [keep.tile([P, ROWS], F32, name="diff%d" % j) for j in range(3)]
-        base = [keep.tile([P, ROWS], F32, name="base%d" % j) for j in range(3)]
+        diff = [keep.tile([P, ROWS], F32, name="diff%d" % j, align_bytes=64) for j in range(3)]
+        base = [keep.tile([P, ROWS], F32, name="base%d" % j, align_bytes=64) for j in range(3)]
         delta = [keep.tile([P, DK], F32, name="delta%d" % j) for j in range(3)]
-        shift = [keep.tile([P, DK], F32, name="shift%d" % j) for j in range(3)]
+        neg_delta = [keep.tile([P, DK], F32, name="neg_delta%d" % j) for j in range(3)]
+        shift_b = [keep.tile([P, DK], F32, name="shift_b%d" % j) for j in range(3)]
+        shift_a = [keep.tile([P, DK], F32, name="shift_a%d" % j) for j in range(3)]
 
-        with tc.tile_pool(name="stage", bufs=2) as stage, tc.tile_pool(name="small", bufs=1) as small:
-            w_sb = []
-            for j in range(3):
-                w_t = small.tile([P, 2 * D], BF16, name="w_sb%d" % j)
-                nc.sync.dma_start(
-                    out=w_t[:].rearrange("p (g k) -> p g k", g=2),
-                    in_=weights[j].rearrange("(g p) k -> p g k", p=P),
+        x_view = x.flatten_outer_dims().rearrange("(t p) k -> p t k", p=P)
+        x_raw = base[2][:].bitcast(BF16)
+        x_grouped = diff[2][:].bitcast(BF16)
+
+        def load_x(c):
+            slot = c % 4
+            nc.sync.dma_start(
+                out=x_raw[:, slot * 2048 : (slot + 1) * 2048].rearrange("p (t k) -> p t k", t=4),
+                in_=x_view[:, 4 * c : 4 * c + 4, :],
+            )
+
+        w_sb = [small.tile([P, 2 * D], BF16, name="w_sb%d" % j) for j in range(3)]
+        t_sb = [small.tile([P, DK], BF16, name="t_sb%d" % j) for j in range(3)]
+        lam_b = small.tile([P, E], BF16, name="lam_b")
+
+        def load_w(j):
+            nc.sync.dma_start(
+                out=w_sb[j][:].rearrange("p (g k) -> p g k", g=2),
+                in_=weights[j].rearrange("(g p) k -> p g k", p=P),
+            )
+
+        load_w(0)
+        for c in range(4):
+            load_x(c)
+        load_w(1)
+        load_w(2)
+        nc.scalar.dma_start(out=lam_b[:], in_=lam.rearrange("a b e -> (a b e)").partition_broadcast(P))
+        for j in range(3):
+            nc.scalar.dma_start(out=t_sb[j][0:DK, :], in_=trops[j])
+            nc.scalar.dma_start(out=t_sb[j][DK:P, :], in_=trops[j])
+
+        def w_prep(j):
+            words = w_sb[j][:].bitcast(F32)
+            bank = psum.tile([P, 512], F32, name="bank", tag="bank")
+            for g in range(2):
+                for u in range(2):
+                    nc.tensor.transpose(
+                        bank[:, u * 256 + g * P : u * 256 + (g + 1) * P],
+                        words[:, g * 256 + u * P : g * 256 + (u + 1) * P],
+                        ident[:],
+                    )
+            gw = small.tile([P, 2 * D], BF16, name="gw%d" % j, align_bytes=64)
+            src = bank[:].rearrange("p (u h i l) -> p i h l u", u=2, h=H, i=2, l=HALF)
+            dst = gw[:].bitcast(F32).rearrange("p (i h l u) -> p i h l u", i=2, h=H, l=HALF, u=2)
+            for i in range(2):
+                nc.vector.tensor_copy(out=dst[:, i], in_=src[:, i])
+            nc.vector.quantize_mx(out=w_codes[j][:].bitcast(FP8X4), scales=w_scales[j][:], in_=gw[:])
+
+        lam_v = lam_b[:].rearrange("p (h i l) -> p h i l", h=H, i=2, l=HALF)
+
+        def t_prep(j):
+            xab = small.tile([P, 2 * P], F32, name="xab%d" % j)
+            for i in range(2):
+                nc.vector.tensor_tensor(
+                    out=xab[:, i * P : (i + 1) * P].rearrange("p (h l) -> p h l", h=H),
+                    in0=t_sb[j][:, i * HALF : (i + 1) * HALF].unsqueeze(1).to_broadcast([P, H, HALF]),
+                    in1=lam_v[:, :, i, :],
+                    op=ALU.subtract,
                 )
-                w_sb.append(w_t)
-            lam_b = small.tile([P, E], BF16, name="lam_b")
-            nc.scalar.dma_start(out=lam_b[:], in_=lam.rearrange("a b e -> (a b e)").partition_broadcast(P))
-            t_sb = []
-            for j in range(3):
-                t_t = small.tile([P, DK], BF16, name="t_sb%d" % j)
-                nc.scalar.dma_start(out=t_t[0:DK, :], in_=trops[j])
-                nc.scalar.dma_start(out=t_t[DK:P, :], in_=trops[j])
-                t_sb.append(t_t)
+            bank = psum.tile([P, 512], F32, name="bank", tag="bank")
+            for i in range(2):
+                nc.tensor.transpose(bank[:, i * P : (i + 1) * P], xab[:, i * P : (i + 1) * P], ident[:])
+            tab = small.tile([P, 2, DK], F32, name="tab%d" % j)
+            nc.vector.tensor_copy(out=tab[:], in_=bank[:, 0 : 2 * P].rearrange("p (i o) -> p i o", i=2)[:, :, 0:DK])
+            nc.vector.tensor_tensor(out=delta[j][:], in0=tab[:, 0, :], in1=tab[:, 1, :], op=ALU.subtract)
+            nc.vector.tensor_scalar(
+                out=delta[j][:], in0=delta[j][:], scalar1=CLAMP, scalar2=-CLAMP, op0=ALU.min, op1=ALU.max
+            )
+            nc.vector.tensor_scalar(
+                out=neg_delta[j][:], in0=delta[j][:], scalar1=-1.0, scalar2=None, op0=ALU.mult
+            )
+            nc.vector.scalar_tensor_tensor(
+                out=shift_b[j][:], in0=tab[:, 0, :], scalar=-CLAMP, in1=tab[:, 1, :], op0=ALU.add, op1=ALU.max
+            )
+            nc.vector.scalar_tensor_tensor(
+                out=shift_a[j][:], in0=tab[:, 1, :], scalar=-CLAMP, in1=tab[:, 0, :], op0=ALU.add, op1=ALU.max
+            )
 
-            for j in range(3):
-                words = w_sb[j][:].bitcast(F32)
+        def x_prep(c):
+            slot = c % 4
+            words = base[2][:, slot * 1024 : (slot + 1) * 1024]
+            grouped = diff[2][:, slot * 1024 : (slot + 1) * 1024]
+            for pr in range(2):
                 bank = psum.tile([P, 512], F32, name="bank", tag="bank")
-                for g in range(2):
+                for tt in range(2):
                     for u in range(2):
+                        t = 2 * pr + tt
                         nc.tensor.transpose(
-                            bank[:, u * 256 + g * P : u * 256 + (g + 1) * P],
-                            words[:, g * 256 + u * P : g * 256 + (u + 1) * P],
+                            bank[:, u * 256 + tt * P : u * 256 + (tt + 1) * P],
+                            words[:, t * 256 + u * P : t * 256 + (u + 1) * P],
                             ident[:],
                         )
-                gw = small.tile([P, 2 * D], BF16, name="gw%d" % j, align_bytes=64)
-                src = bank[:].rearrange("p (u h i l) -> p i h l u", u=2, h=H, i=2, l=HALF)
-                dst = gw[:].bitcast(F32).rearrange("p (i h l u) -> p i h l u", i=2, h=H, l=HALF, u=2)
-                for i in range(2):
-                    nc.vector.tensor_copy(out=dst[:, i], in_=src[:, i])
-                nc.vector.quantize_mx(out=w_codes[j][:].bitcast(FP8X4), scales=w_scales[j][:], in_=gw[:])
+                dst = grouped[:, pr * 512 : (pr + 1) * 512].rearrange("p (r u) -> p r u", u=2)
+                src = bank[:].rearrange("p (u r) -> p r u", u=2)
+                if pr == 0:
+                    nc.vector.tensor_copy(out=dst, in_=src)
+                else:
+                    nc.scalar.copy(out=dst, in_=src)
+            nc.vector.quantize_mx(
+                out=x_codes[:, c * PIECE : (c + 1) * PIECE].bitcast(FP8X4),
+                scales=x_scales[:, c * PIECE : (c + 1) * PIECE],
+                in_=x_grouped[:, slot * 2048 : (slot + 1) * 2048],
+            )
 
-            lam_v = lam_b[:].rearrange("p (h i l) -> p h i l", h=H, i=2, l=HALF)
-            for j in range(3):
-                xab = small.tile([P, 2 * P], F32, name="xab%d" % j)
-                for i in range(2):
-                    nc.vector.tensor_tensor(
-                        out=xab[:, i * P : (i + 1) * P].rearrange("p (h l) -> p h l", h=H),
-                        in0=t_sb[j][:, i * HALF : (i + 1) * HALF].unsqueeze(1).to_broadcast([P, H, HALF]),
-                        in1=lam_v[:, :, i, :],
-                        op=ALU.subtract,
-                    )
-                bank = psum.tile([P, 512], F32, name="bank", tag="bank")
-                for i in range(2):
-                    nc.tensor.transpose(bank[:, i * P : (i + 1) * P], xab[:, i * P : (i + 1) * P], ident[:])
-                tab = small.tile([P, 2, DK], F32, name="tab%d" % j)
-                nc.vector.tensor_copy(
-                    out=tab[:], in_=bank[:, 0 : 2 * P].rearrange("p (i o) -> p i o", i=2)[:, :, 0:DK]
-                )
-                nc.vector.tensor_tensor(out=delta[j][:], in0=tab[:, 0, :], in1=tab[:, 1, :], op=ALU.subtract)
-                nc.vector.tensor_scalar(
-                    out=delta[j][:], in0=delta[j][:], scalar1=CLAMP, scalar2=-CLAMP, op0=ALU.min, op1=ALU.max
-                )
-                nc.vector.scalar_tensor_tensor(
-                    out=shift[j][:], in0=tab[:, 0, :], scalar=-CLAMP, in1=tab[:, 1, :], op0=ALU.add, op1=ALU.max
-                )
-
-            x_view = x.flatten_outer_dims().rearrange("(t p) k -> p t k", p=P)
-            for c in range(4):
-                xs = stage.tile([P, 8 * D], BF16, name="xs", tag="xs")
-                nc.sync.dma_start(
-                    out=xs[:].rearrange("p (t k) -> p t k", t=8), in_=x_view[:, 8 * c : 8 * c + 8, :]
-                )
-                words = xs[:].bitcast(F32)
-                gx = stage.tile([P, 8 * D], BF16, name="gx", tag="gx", align_bytes=64)
-                gx_words = gx[:].bitcast(F32)
-                for pr in range(4):
-                    bank = psum.tile([P, 512], F32, name="bank", tag="bank")
-                    for tt in range(2):
-                        for u in range(2):
-                            t = 2 * pr + tt
-                            nc.tensor.transpose(
-                                bank[:, u * 256 + tt * P : u * 256 + (tt + 1) * P],
-                                words[:, t * 256 + u * P : t * 256 + (u + 1) * P],
-                                ident[:],
-                            )
-                    dst = gx_words[:, pr * 512 : (pr + 1) * 512].rearrange("p (r u) -> p r u", u=2)
-                    src = bank[:].rearrange("p (u r) -> p r u", u=2)
-                    if pr % 2 == 0:
-                        nc.vector.tensor_copy(out=dst, in_=src)
-                    else:
-                        nc.scalar.copy(out=dst, in_=src)
-                nc.vector.quantize_mx(
-                    out=x_codes[:, c * 1024 : (c + 1) * 1024].bitcast(FP8X4),
-                    scales=x_scales[:, c * 1024 : (c + 1) * 1024],
-                    in_=gx[:],
-                )
-
-        relu_pool = ctx.enter_context(tc.tile_pool(name="relu_pool", bufs=3))
-        base_pool = ctx.enter_context(tc.tile_pool(name="base_pool", bufs=3))
-        y_pool = ctx.enter_context(tc.tile_pool(name="y_pool", bufs=2))
-
-        def prep_piece(j, c):
+        def prep_piece(j, c, early):
             cols = slice(c * PIECE, (c + 1) * PIECE)
             for i in range(2):
                 bank = psum.tile([P, 512], F32, name="bank", tag="bank")
@@ -159,50 +177,80 @@ def tile_tropicalattention_pa_t_kernel(
                     start=True,
                     stop=True,
                 )
-                one_plus = tmp.tile([P, PIECE], F32, name="one_plus", tag="one_plus")
-                nc.vector.tensor_scalar(
-                    out=one_plus[:], in0=bank[:], scalar1=0.0, scalar2=1.0, op0=ALU.max, op1=ALU.add
-                )
+                positive = tmp.tile([P, PIECE], F32, name="positive", tag="positive")
+                if early:
+                    nc.vector.tensor_scalar(out=positive[:], in0=bank[:], scalar1=0.0, scalar2=None, op0=ALU.max)
+                else:
+                    nc.scalar.activation(out=positive[:], in_=bank[:], func=ACT.Relu)
                 target = diff[j] if i == 0 else base[j]
-                nc.scalar.activation(out=target[:, cols], in_=one_plus[:], func=ACT.Ln)
+                nc.scalar.activation(out=target[:, cols], in_=positive[:], func=ACT.Ln, bias=ones[:, 0:1], scale=1.0)
             nc.vector.tensor_tensor(out=diff[j][:, cols], in0=diff[j][:, cols], in1=base[j][:, cols], op=ALU.subtract)
 
+        w_prep(0)
+        t_prep(0)
+        for c in range(4):
+            x_prep(c)
+            prep_piece(0, c, True)
+
+        jobs = {}
+
+        def add_job(at, job, args):
+            jobs[at] = jobs.get(at, []) + [(job, args)]
+
+        for c in range(4, 8):
+            add_job(0, load_x, (c,))
+            add_job(c - 3, x_prep, (c,))
+        add_job(9, w_prep, (1,))
+        add_job(10, t_prep, (1,))
+        add_job(11, w_prep, (2,))
+        add_job(12, t_prep, (2,))
         pieces = [(j, c) for j in range(3) for c in range(ROWS // PIECE)]
-        for k in range(4):
-            prep_piece(*pieces[k])
-        next_piece = 4
+        for m in range(len(pieces) - 4):
+            add_job(16 * m + 6, prep_piece, (pieces[4 + m][0], pieces[4 + m][1], False))
 
         step = 0
         for j in range(3):
             for chunk in range(ROWS // CHUNK):
-                rows = slice(chunk * CHUNK, (chunk + 1) * CHUNK)
+                r0 = chunk * CHUNK
                 y = y_pool.tile([P, TILES, H, DK], F32, name="y", tag="y")
                 for o in range(DK):
-                    if step % 16 == 0 and next_piece < len(pieces):
-                        prep_piece(*pieces[next_piece])
-                        next_piece += 1
+                    for job, args in jobs.get(step, []):
+                        job(*args)
                     step += 1
+                    n_merged = MERGED[o % 2]
+                    split = CHUNK - n_merged * P
                     gain = relu_pool.tile([P, CHUNK], F32, name="gain", tag="gain")
                     nc.scalar.activation(
-                        out=gain[:], in_=diff[j][:, rows], func=ACT.Relu, bias=delta[j][:, o : o + 1], scale=1.0
+                        out=gain[:, 0:split], in_=diff[j][:, r0 : r0 + split], func=ACT.Relu,
+                        bias=delta[j][:, o : o + 1], scale=1.0,
                     )
                     floor = base_pool.tile([P, CHUNK], F32, name="floor", tag="floor")
+                    nc.scalar.activation(
+                        out=floor[:, split:CHUNK], in_=base[j][:, r0 + split : r0 + CHUNK], func=ACT.Identity,
+                        bias=shift_a[j][:, o : o + 1], scale=1.0,
+                    )
                     nc.gpsimd.tensor_scalar(
-                        out=floor[:], in0=base[j][:, rows], scalar1=shift[j][:, o : o + 1], scalar2=1.0,
-                        op0=ALU.add, op1=ALU.mult,
+                        out=floor[:, 0:split], in0=base[j][:, r0 : r0 + split], scalar1=shift_b[j][:, o : o + 1],
+                        scalar2=1.0, op0=ALU.add, op1=ALU.mult,
+                    )
+                    nc.vector.scalar_tensor_tensor(
+                        out=gain[:, split:CHUNK], in0=diff[j][:, r0 + split : r0 + CHUNK],
+                        scalar=neg_delta[j][:, o : o + 1], in1=floor[:, split:CHUNK], op0=ALU.max, op1=ALU.add,
                     )
                     for q in range(TILES // 4):
                         bank = psum.tile([P, 512], F32, name="bank", tag="bank")
                         for s in range(4):
                             t = 4 * q + s
+                            whole = t * P >= split
                             nc.tensor.matmul(
                                 out=bank[:, s * P : (s + 1) * P], lhsT=gain[:, t * P : (t + 1) * P], rhs=ident[:],
-                                is_transpose=True, start=True, stop=False,
+                                is_transpose=True, start=True, stop=whole,
                             )
-                            nc.tensor.matmul(
-                                out=bank[:, s * P : (s + 1) * P], lhsT=floor[:, t * P : (t + 1) * P], rhs=ident[:],
-                                is_transpose=True, start=False, stop=True,
-                            )
+                            if not whole:
+                                nc.tensor.matmul(
+                                    out=bank[:, s * P : (s + 1) * P], lhsT=floor[:, t * P : (t + 1) * P],
+                                    rhs=ident[:], is_transpose=True, start=False, stop=True,
+                                )
                         nc.vector.tensor_reduce(
                             out=y[:, 4 * q : 4 * q + 4, :, o],
                             in_=bank[:].rearrange("p (s h l) -> p s h l", s=4, h=H, l=HALF),

@@ -21,7 +21,8 @@ CHUNK = 2048
 TILES = CHUNK // P
 PIECE = 512
 CLAMP = 128.0
-MERGED = (1, 2)
+MERGED = 2
+SPLIT = CHUNK - MERGED * P
 
 FLOPS = 2 * ROWS * D * 3 * E + 2 * 3 * ROWS * H * DK * DK
 
@@ -37,12 +38,9 @@ def tile_tropicalattention_pa_t_kernel(
     with ExitStack() as ctx:
         const = ctx.enter_context(tc.tile_pool(name="const", bufs=1))
         keep = ctx.enter_context(tc.tile_pool(name="keep", bufs=1))
-        small = ctx.enter_context(tc.tile_pool(name="small", bufs=1))
         tmp = ctx.enter_context(tc.tile_pool(name="tmp", bufs=3))
-        relu_pool = ctx.enter_context(tc.tile_pool(name="relu_pool", bufs=3))
-        base_pool = ctx.enter_context(tc.tile_pool(name="base_pool", bufs=3))
-        y_pool = ctx.enter_context(tc.tile_pool(name="y_pool", bufs=2))
-        psum = ctx.enter_context(tc.psum_pool(name="psum", bufs=8))
+        psum = ctx.enter_context(tc.psum_pool(name="psum", bufs=6))
+        psum_keep = ctx.enter_context(tc.psum_pool(name="psum_keep", bufs=2))
 
         ident = const.tile([P, P], F32, name="ident")
         make_identity(nc, ident[:])
@@ -53,116 +51,105 @@ def tile_tropicalattention_pa_t_kernel(
         x_scales = keep.tile([P, ROWS], U8, name="x_scales", align_bytes=64)
         w_codes = [keep.tile([P, 2 * P], U32, name="w_codes%d" % j, align_bytes=64) for j in range(3)]
         w_scales = [keep.tile([P, 2 * P], U8, name="w_scales%d" % j, align_bytes=64) for j in range(3)]
-        diff = [keep.tile([P, ROWS], F32, name="diff%d" % j, align_bytes=64) for j in range(3)]
-        base = [keep.tile([P, ROWS], F32, name="base%d" % j, align_bytes=64) for j in range(3)]
+        diff = [keep.tile([P, ROWS], F32, name="diff%d" % j) for j in range(3)]
+        base = [keep.tile([P, ROWS], F32, name="base%d" % j) for j in range(3)]
         delta = [keep.tile([P, DK], F32, name="delta%d" % j) for j in range(3)]
-        neg_delta = [keep.tile([P, DK], F32, name="neg_delta%d" % j) for j in range(3)]
-        shift_b = [keep.tile([P, DK], F32, name="shift_b%d" % j) for j in range(3)]
-        shift_a = [keep.tile([P, DK], F32, name="shift_a%d" % j) for j in range(3)]
+        shift = [keep.tile([P, DK], F32, name="shift%d" % j) for j in range(3)]
 
-        x_view = x.flatten_outer_dims().rearrange("(t p) k -> p t k", p=P)
-        x_raw = base[2][:].bitcast(BF16)
-        x_grouped = diff[2][:].bitcast(BF16)
-
-        def load_x(c):
-            slot = c % 4
-            nc.sync.dma_start(
-                out=x_raw[:, slot * 2048 : (slot + 1) * 2048].rearrange("p (t k) -> p t k", t=4),
-                in_=x_view[:, 4 * c : 4 * c + 4, :],
-            )
-
-        w_sb = [small.tile([P, 2 * D], BF16, name="w_sb%d" % j) for j in range(3)]
-        t_sb = [small.tile([P, DK], BF16, name="t_sb%d" % j) for j in range(3)]
-        lam_b = small.tile([P, E], BF16, name="lam_b")
-
-        def load_w(j):
-            nc.sync.dma_start(
-                out=w_sb[j][:].rearrange("p (g k) -> p g k", g=2),
-                in_=weights[j].rearrange("(g p) k -> p g k", p=P),
-            )
-
-        load_w(0)
-        for c in range(4):
-            load_x(c)
-        load_w(1)
-        load_w(2)
-        nc.scalar.dma_start(out=lam_b[:], in_=lam.rearrange("a b e -> (a b e)").partition_broadcast(P))
-        for j in range(3):
-            nc.scalar.dma_start(out=t_sb[j][0:DK, :], in_=trops[j])
-            nc.scalar.dma_start(out=t_sb[j][DK:P, :], in_=trops[j])
-
-        def w_prep(j):
-            words = w_sb[j][:].bitcast(F32)
-            bank = psum.tile([P, 512], F32, name="bank", tag="bank")
-            for g in range(2):
-                for u in range(2):
-                    nc.tensor.transpose(
-                        bank[:, u * 256 + g * P : u * 256 + (g + 1) * P],
-                        words[:, g * 256 + u * P : g * 256 + (u + 1) * P],
-                        ident[:],
-                    )
-            gw = small.tile([P, 2 * D], BF16, name="gw%d" % j, align_bytes=64)
-            src = bank[:].rearrange("p (u h i l) -> p i h l u", u=2, h=H, i=2, l=HALF)
-            dst = gw[:].bitcast(F32).rearrange("p (i h l u) -> p i h l u", i=2, h=H, l=HALF, u=2)
-            for i in range(2):
-                nc.vector.tensor_copy(out=dst[:, i], in_=src[:, i])
-            nc.vector.quantize_mx(out=w_codes[j][:].bitcast(FP8X4), scales=w_scales[j][:], in_=gw[:])
-
-        lam_v = lam_b[:].rearrange("p (h i l) -> p h i l", h=H, i=2, l=HALF)
-
-        def t_prep(j):
-            xab = small.tile([P, 2 * P], F32, name="xab%d" % j)
-            for i in range(2):
-                nc.vector.tensor_tensor(
-                    out=xab[:, i * P : (i + 1) * P].rearrange("p (h l) -> p h l", h=H),
-                    in0=t_sb[j][:, i * HALF : (i + 1) * HALF].unsqueeze(1).to_broadcast([P, H, HALF]),
-                    in1=lam_v[:, :, i, :],
-                    op=ALU.subtract,
+        with tc.tile_pool(name="stage", bufs=2) as stage, tc.tile_pool(name="small", bufs=1) as small:
+            w_sb = []
+            for j in range(3):
+                w_t = small.tile([P, 2 * D], BF16, name="w_sb%d" % j)
+                nc.sync.dma_start(
+                    out=w_t[:].rearrange("p (g k) -> p g k", g=2),
+                    in_=weights[j].rearrange("(g p) k -> p g k", p=P),
                 )
-            bank = psum.tile([P, 512], F32, name="bank", tag="bank")
-            for i in range(2):
-                nc.tensor.transpose(bank[:, i * P : (i + 1) * P], xab[:, i * P : (i + 1) * P], ident[:])
-            tab = small.tile([P, 2, DK], F32, name="tab%d" % j)
-            nc.vector.tensor_copy(out=tab[:], in_=bank[:, 0 : 2 * P].rearrange("p (i o) -> p i o", i=2)[:, :, 0:DK])
-            nc.vector.tensor_tensor(out=delta[j][:], in0=tab[:, 0, :], in1=tab[:, 1, :], op=ALU.subtract)
-            nc.vector.tensor_scalar(
-                out=delta[j][:], in0=delta[j][:], scalar1=CLAMP, scalar2=-CLAMP, op0=ALU.min, op1=ALU.max
-            )
-            nc.vector.tensor_scalar(
-                out=neg_delta[j][:], in0=delta[j][:], scalar1=-1.0, scalar2=None, op0=ALU.mult
-            )
-            nc.vector.scalar_tensor_tensor(
-                out=shift_b[j][:], in0=tab[:, 0, :], scalar=-CLAMP, in1=tab[:, 1, :], op0=ALU.add, op1=ALU.max
-            )
-            nc.vector.scalar_tensor_tensor(
-                out=shift_a[j][:], in0=tab[:, 1, :], scalar=-CLAMP, in1=tab[:, 0, :], op0=ALU.add, op1=ALU.max
-            )
+                w_sb.append(w_t)
+            lam_b = small.tile([P, E], BF16, name="lam_b")
+            nc.scalar.dma_start(out=lam_b[:], in_=lam.rearrange("a b e -> (a b e)").partition_broadcast(P))
+            t_sb = []
+            for j in range(3):
+                t_t = small.tile([P, DK], BF16, name="t_sb%d" % j)
+                nc.scalar.dma_start(out=t_t[0:DK, :], in_=trops[j])
+                nc.scalar.dma_start(out=t_t[DK:P, :], in_=trops[j])
+                t_sb.append(t_t)
 
-        def x_prep(c):
-            slot = c % 4
-            words = base[2][:, slot * 1024 : (slot + 1) * 1024]
-            grouped = diff[2][:, slot * 1024 : (slot + 1) * 1024]
-            for pr in range(2):
+            for j in range(3):
+                words = w_sb[j][:].bitcast(F32)
                 bank = psum.tile([P, 512], F32, name="bank", tag="bank")
-                for tt in range(2):
+                for g in range(2):
                     for u in range(2):
-                        t = 2 * pr + tt
                         nc.tensor.transpose(
-                            bank[:, u * 256 + tt * P : u * 256 + (tt + 1) * P],
-                            words[:, t * 256 + u * P : t * 256 + (u + 1) * P],
+                            bank[:, u * 256 + g * P : u * 256 + (g + 1) * P],
+                            words[:, g * 256 + u * P : g * 256 + (u + 1) * P],
                             ident[:],
                         )
-                dst = grouped[:, pr * 512 : (pr + 1) * 512].rearrange("p (r u) -> p r u", u=2)
-                src = bank[:].rearrange("p (u r) -> p r u", u=2)
-                if pr == 0:
-                    nc.vector.tensor_copy(out=dst, in_=src)
-                else:
-                    nc.scalar.copy(out=dst, in_=src)
-            nc.vector.quantize_mx(
-                out=x_codes[:, c * PIECE : (c + 1) * PIECE].bitcast(FP8X4),
-                scales=x_scales[:, c * PIECE : (c + 1) * PIECE],
-                in_=x_grouped[:, slot * 2048 : (slot + 1) * 2048],
-            )
+                gw = small.tile([P, 2 * D], BF16, name="gw%d" % j, align_bytes=64)
+                src = bank[:].rearrange("p (u h i l) -> p i h l u", u=2, h=H, i=2, l=HALF)
+                dst = gw[:].bitcast(F32).rearrange("p (i h l u) -> p i h l u", i=2, h=H, l=HALF, u=2)
+                for i in range(2):
+                    nc.vector.tensor_copy(out=dst[:, i], in_=src[:, i])
+                nc.vector.quantize_mx(out=w_codes[j][:].bitcast(FP8X4), scales=w_scales[j][:], in_=gw[:])
+
+            lam_v = lam_b[:].rearrange("p (h i l) -> p h i l", h=H, i=2, l=HALF)
+            for j in range(3):
+                xab = small.tile([P, 2 * P], F32, name="xab%d" % j)
+                for i in range(2):
+                    nc.vector.tensor_tensor(
+                        out=xab[:, i * P : (i + 1) * P].rearrange("p (h l) -> p h l", h=H),
+                        in0=t_sb[j][:, i * HALF : (i + 1) * HALF].unsqueeze(1).to_broadcast([P, H, HALF]),
+                        in1=lam_v[:, :, i, :],
+                        op=ALU.subtract,
+                    )
+                bank = psum.tile([P, 512], F32, name="bank", tag="bank")
+                for i in range(2):
+                    nc.tensor.transpose(bank[:, i * P : (i + 1) * P], xab[:, i * P : (i + 1) * P], ident[:])
+                tab = small.tile([P, 2, DK], F32, name="tab%d" % j)
+                nc.vector.tensor_copy(
+                    out=tab[:], in_=bank[:, 0 : 2 * P].rearrange("p (i o) -> p i o", i=2)[:, :, 0:DK]
+                )
+                nc.vector.tensor_tensor(out=delta[j][:], in0=tab[:, 0, :], in1=tab[:, 1, :], op=ALU.subtract)
+                nc.vector.tensor_scalar(
+                    out=delta[j][:], in0=delta[j][:], scalar1=CLAMP, scalar2=-CLAMP, op0=ALU.min, op1=ALU.max
+                )
+                nc.vector.scalar_tensor_tensor(
+                    out=shift[j][:], in0=tab[:, 0, :], scalar=-CLAMP, in1=tab[:, 1, :], op0=ALU.add, op1=ALU.max
+                )
+
+            x_view = x.flatten_outer_dims().rearrange("(t p) k -> p t k", p=P)
+            for c in range(4):
+                xs = stage.tile([P, 8 * D], BF16, name="xs", tag="xs")
+                nc.sync.dma_start(
+                    out=xs[:].rearrange("p (t k) -> p t k", t=8), in_=x_view[:, 8 * c : 8 * c + 8, :]
+                )
+                words = xs[:].bitcast(F32)
+                gx = stage.tile([P, 8 * D], BF16, name="gx", tag="gx", align_bytes=64)
+                gx_words = gx[:].bitcast(F32)
+                for pr in range(4):
+                    bank = psum.tile([P, 512], F32, name="bank", tag="bank")
+                    for tt in range(2):
+                        for u in range(2):
+                            t = 2 * pr + tt
+                            nc.tensor.transpose(
+                                bank[:, u * 256 + tt * P : u * 256 + (tt + 1) * P],
+                                words[:, t * 256 + u * P : t * 256 + (u + 1) * P],
+                                ident[:],
+                            )
+                    dst = gx_words[:, pr * 512 : (pr + 1) * 512].rearrange("p (r u) -> p r u", u=2)
+                    src = bank[:].rearrange("p (u r) -> p r u", u=2)
+                    if pr % 2 == 0:
+                        nc.vector.tensor_copy(out=dst, in_=src)
+                    else:
+                        nc.scalar.copy(out=dst, in_=src)
+                nc.vector.quantize_mx(
+                    out=x_codes[:, c * 1024 : (c + 1) * 1024].bitcast(FP8X4),
+                    scales=x_scales[:, c * 1024 : (c + 1) * 1024],
+                    in_=gx[:],
+                )
+
+        relu_pool = ctx.enter_context(tc.tile_pool(name="relu_pool", bufs=3))
+        base_pool = ctx.enter_context(tc.tile_pool(name="base_pool", bufs=3))
+        y_pool = ctx.enter_context(tc.tile_pool(name="y_pool", bufs=2))
 
         def prep_piece(j, c, early):
             cols = slice(c * PIECE, (c + 1) * PIECE)
@@ -184,64 +171,59 @@ def tile_tropicalattention_pa_t_kernel(
                     nc.scalar.activation(out=positive[:], in_=bank[:], func=ACT.Relu)
                 target = diff[j] if i == 0 else base[j]
                 nc.scalar.activation(out=target[:, cols], in_=positive[:], func=ACT.Ln, bias=ones[:, 0:1], scale=1.0)
-            nc.vector.tensor_tensor(out=diff[j][:, cols], in0=diff[j][:, cols], in1=base[j][:, cols], op=ALU.subtract)
+            engine = nc.vector if early else nc.gpsimd
+            engine.tensor_tensor(out=diff[j][:, cols], in0=diff[j][:, cols], in1=base[j][:, cols], op=ALU.subtract)
 
-        w_prep(0)
-        t_prep(0)
-        for c in range(4):
-            x_prep(c)
-            prep_piece(0, c, True)
+        def resident_base(j, chunk):
+            c0 = chunk * CHUNK + SPLIT
+            bank = psum.tile([P, 512], F32, name="bank", tag="bank")
+            for s in range(MERGED):
+                nc.tensor.transpose(bank[:, s * P : (s + 1) * P], base[j][:, c0 + s * P : c0 + (s + 1) * P], ident[:])
+            turned = tmp.tile([P, MERGED * P], F32, name="turned", tag="turned")
+            nc.scalar.copy(out=turned[:], in_=bank[:, 0 : MERGED * P])
+            kept = psum_keep.tile([P, 512], F32, name="kept", tag="kept")
+            for s in range(MERGED):
+                nc.tensor.transpose(kept[:, s * P : (s + 1) * P], turned[:, s * P : (s + 1) * P], ident[:])
+            return kept
 
-        jobs = {}
-
-        def add_job(at, job, args):
-            jobs[at] = jobs.get(at, []) + [(job, args)]
-
-        for c in range(4, 8):
-            add_job(0, load_x, (c,))
-            add_job(c - 3, x_prep, (c,))
-        add_job(9, w_prep, (1,))
-        add_job(10, t_prep, (1,))
-        add_job(11, w_prep, (2,))
-        add_job(12, t_prep, (2,))
         pieces = [(j, c) for j in range(3) for c in range(ROWS // PIECE)]
-        for m in range(len(pieces) - 4):
-            add_job(16 * m + 6, prep_piece, (pieces[4 + m][0], pieces[4 + m][1], False))
+        for k in range(4):
+            prep_piece(pieces[k][0], pieces[k][1], True)
+        next_piece = 4
+        chunks = [(j, chunk) for j in range(3) for chunk in range(ROWS // CHUNK)]
+        kept_next = resident_base(0, 0)
 
         step = 0
         for j in range(3):
             for chunk in range(ROWS // CHUNK):
-                r0 = chunk * CHUNK
+                rows = slice(chunk * CHUNK, (chunk + 1) * CHUNK)
                 y = y_pool.tile([P, TILES, H, DK], F32, name="y", tag="y")
+                kept = kept_next
                 for o in range(DK):
-                    for job, args in jobs.get(step, []):
-                        job(*args)
+                    if step % 16 == 0 and next_piece < len(pieces):
+                        prep_piece(pieces[next_piece][0], pieces[next_piece][1], False)
+                        next_piece += 1
+                    if o == DK - 8 and step // DK + 1 < len(chunks):
+                        kept_next = resident_base(*chunks[step // DK + 1])
                     step += 1
-                    n_merged = MERGED[o % 2]
-                    split = CHUNK - n_merged * P
                     gain = relu_pool.tile([P, CHUNK], F32, name="gain", tag="gain")
                     nc.scalar.activation(
-                        out=gain[:, 0:split], in_=diff[j][:, r0 : r0 + split], func=ACT.Relu,
-                        bias=delta[j][:, o : o + 1], scale=1.0,
+                        out=gain[:], in_=diff[j][:, rows], func=ACT.Relu, bias=delta[j][:, o : o + 1], scale=1.0
                     )
-                    floor = base_pool.tile([P, CHUNK], F32, name="floor", tag="floor")
-                    nc.scalar.activation(
-                        out=floor[:, split:CHUNK], in_=base[j][:, r0 + split : r0 + CHUNK], func=ACT.Identity,
-                        bias=shift_a[j][:, o : o + 1], scale=1.0,
-                    )
+                    floor = base_pool.tile([P, SPLIT], F32, name="floor", tag="floor")
                     nc.gpsimd.tensor_scalar(
-                        out=floor[:, 0:split], in0=base[j][:, r0 : r0 + split], scalar1=shift_b[j][:, o : o + 1],
-                        scalar2=1.0, op0=ALU.add, op1=ALU.mult,
+                        out=floor[:], in0=base[j][:, chunk * CHUNK : chunk * CHUNK + SPLIT],
+                        scalar1=shift[j][:, o : o + 1], scalar2=1.0, op0=ALU.add, op1=ALU.mult,
                     )
                     nc.vector.scalar_tensor_tensor(
-                        out=gain[:, split:CHUNK], in0=diff[j][:, r0 + split : r0 + CHUNK],
-                        scalar=neg_delta[j][:, o : o + 1], in1=floor[:, split:CHUNK], op0=ALU.max, op1=ALU.add,
+                        out=gain[:, SPLIT:CHUNK], in0=gain[:, SPLIT:CHUNK], scalar=shift[j][:, o : o + 1],
+                        in1=kept[:, 0 : MERGED * P], op0=ALU.add, op1=ALU.add,
                     )
                     for q in range(TILES // 4):
                         bank = psum.tile([P, 512], F32, name="bank", tag="bank")
                         for s in range(4):
                             t = 4 * q + s
-                            whole = t * P >= split
+                            whole = t * P >= SPLIT
                             nc.tensor.matmul(
                                 out=bank[:, s * P : (s + 1) * P], lhsT=gain[:, t * P : (t + 1) * P], rhs=ident[:],
                                 is_transpose=True, start=True, stop=whole,

@@ -21,8 +21,6 @@ CHUNK = 2048
 TILES = CHUNK // P
 PIECE = 512
 CLAMP = 128.0
-MERGED = 2
-SPLIT = CHUNK - MERGED * P
 
 FLOPS = 2 * ROWS * D * 3 * E + 2 * 3 * ROWS * H * DK * DK
 
@@ -39,13 +37,10 @@ def tile_tropicalattention_pa_t_kernel(
         const = ctx.enter_context(tc.tile_pool(name="const", bufs=1))
         keep = ctx.enter_context(tc.tile_pool(name="keep", bufs=1))
         tmp = ctx.enter_context(tc.tile_pool(name="tmp", bufs=3))
-        psum = ctx.enter_context(tc.psum_pool(name="psum", bufs=6))
-        psum_keep = ctx.enter_context(tc.psum_pool(name="psum_keep", bufs=2))
+        psum = ctx.enter_context(tc.psum_pool(name="psum", bufs=8))
 
         ident = const.tile([P, P], F32, name="ident")
         make_identity(nc, ident[:])
-        ones = const.tile([P, 1], F32, name="ones")
-        nc.vector.memset(ones[:], 1.0)
 
         x_codes = keep.tile([P, ROWS], U32, name="x_codes", align_bytes=64)
         x_scales = keep.tile([P, ROWS], U8, name="x_scales", align_bytes=64)
@@ -151,7 +146,7 @@ def tile_tropicalattention_pa_t_kernel(
         base_pool = ctx.enter_context(tc.tile_pool(name="base_pool", bufs=3))
         y_pool = ctx.enter_context(tc.tile_pool(name="y_pool", bufs=2))
 
-        def prep_piece(j, c, early):
+        def prep_piece(j, c):
             cols = slice(c * PIECE, (c + 1) * PIECE)
             for i in range(2):
                 bank = psum.tile([P, 512], F32, name="bank", tag="bank")
@@ -164,81 +159,61 @@ def tile_tropicalattention_pa_t_kernel(
                     start=True,
                     stop=True,
                 )
-                positive = tmp.tile([P, PIECE], F32, name="positive", tag="positive")
-                if early:
-                    nc.vector.tensor_scalar(out=positive[:], in0=bank[:], scalar1=0.0, scalar2=None, op0=ALU.max)
-                else:
-                    nc.scalar.activation(out=positive[:], in_=bank[:], func=ACT.Relu)
+                one_plus = tmp.tile([P, PIECE], F32, name="one_plus", tag="one_plus")
+                nc.vector.tensor_scalar(
+                    out=one_plus[:], in0=bank[:], scalar1=0.0, scalar2=1.0, op0=ALU.max, op1=ALU.add
+                )
                 target = diff[j] if i == 0 else base[j]
-                nc.scalar.activation(out=target[:, cols], in_=positive[:], func=ACT.Ln, bias=ones[:, 0:1], scale=1.0)
-            engine = nc.vector if early else nc.gpsimd
-            engine.tensor_tensor(out=diff[j][:, cols], in0=diff[j][:, cols], in1=base[j][:, cols], op=ALU.subtract)
-
-        def resident_base(j, chunk):
-            c0 = chunk * CHUNK + SPLIT
-            bank = psum.tile([P, 512], F32, name="bank", tag="bank")
-            for s in range(MERGED):
-                nc.tensor.transpose(bank[:, s * P : (s + 1) * P], base[j][:, c0 + s * P : c0 + (s + 1) * P], ident[:])
-            turned = tmp.tile([P, MERGED * P], F32, name="turned", tag="turned")
-            nc.scalar.copy(out=turned[:], in_=bank[:, 0 : MERGED * P])
-            kept = psum_keep.tile([P, 512], F32, name="kept", tag="kept")
-            for s in range(MERGED):
-                nc.tensor.transpose(kept[:, s * P : (s + 1) * P], turned[:, s * P : (s + 1) * P], ident[:])
-            return kept
+                nc.scalar.activation(out=target[:, cols], in_=one_plus[:], func=ACT.Ln)
+            nc.vector.tensor_tensor(out=diff[j][:, cols], in0=diff[j][:, cols], in1=base[j][:, cols], op=ALU.subtract)
 
         pieces = [(j, c) for j in range(3) for c in range(ROWS // PIECE)]
         for k in range(4):
-            prep_piece(pieces[k][0], pieces[k][1], True)
+            prep_piece(*pieces[k])
         next_piece = 4
-        chunks = [(j, chunk) for j in range(3) for chunk in range(ROWS // CHUNK)]
-        kept_next = resident_base(0, 0)
 
         step = 0
         for j in range(3):
             for chunk in range(ROWS // CHUNK):
                 rows = slice(chunk * CHUNK, (chunk + 1) * CHUNK)
                 y = y_pool.tile([P, TILES, H, DK], F32, name="y", tag="y")
-                kept = kept_next
                 for o in range(DK):
                     if step % 16 == 0 and next_piece < len(pieces):
-                        prep_piece(pieces[next_piece][0], pieces[next_piece][1], False)
+                        prep_piece(*pieces[next_piece])
                         next_piece += 1
-                    if o == DK - 8 and step // DK + 1 < len(chunks):
-                        kept_next = resident_base(*chunks[step // DK + 1])
                     step += 1
                     gain = relu_pool.tile([P, CHUNK], F32, name="gain", tag="gain")
                     nc.scalar.activation(
                         out=gain[:], in_=diff[j][:, rows], func=ACT.Relu, bias=delta[j][:, o : o + 1], scale=1.0
                     )
-                    floor = base_pool.tile([P, SPLIT], F32, name="floor", tag="floor")
+                    floor = base_pool.tile([P, CHUNK], F32, name="floor", tag="floor")
                     nc.gpsimd.tensor_scalar(
-                        out=floor[:], in0=base[j][:, chunk * CHUNK : chunk * CHUNK + SPLIT],
-                        scalar1=shift[j][:, o : o + 1], scalar2=1.0, op0=ALU.add, op1=ALU.mult,
+                        out=floor[:], in0=base[j][:, rows], scalar1=shift[j][:, o : o + 1], scalar2=1.0,
+                        op0=ALU.add, op1=ALU.mult,
                     )
-                    nc.vector.scalar_tensor_tensor(
-                        out=gain[:, SPLIT:CHUNK], in0=gain[:, SPLIT:CHUNK], scalar=shift[j][:, o : o + 1],
-                        in1=kept[:, 0 : MERGED * P], op0=ALU.add, op1=ALU.add,
-                    )
-                    for q in range(TILES // 4):
-                        bank = psum.tile([P, 512], F32, name="bank", tag="bank")
+                    for q2 in range(TILES // 8):
+                        banks = [psum.tile([P, 512], F32, name="bank", tag="bank") for e in range(2)]
                         for s in range(4):
-                            t = 4 * q + s
-                            whole = t * P >= SPLIT
-                            nc.tensor.matmul(
-                                out=bank[:, s * P : (s + 1) * P], lhsT=gain[:, t * P : (t + 1) * P], rhs=ident[:],
-                                is_transpose=True, start=True, stop=whole,
-                            )
-                            if not whole:
+                            for e in range(2):
+                                t = 4 * (2 * q2 + e) + s
                                 nc.tensor.matmul(
-                                    out=bank[:, s * P : (s + 1) * P], lhsT=floor[:, t * P : (t + 1) * P],
+                                    out=banks[e][:, s * P : (s + 1) * P], lhsT=gain[:, t * P : (t + 1) * P],
+                                    rhs=ident[:], is_transpose=True, start=True, stop=False,
+                                )
+                            for e in range(2):
+                                t = 4 * (2 * q2 + e) + s
+                                nc.tensor.matmul(
+                                    out=banks[e][:, s * P : (s + 1) * P], lhsT=floor[:, t * P : (t + 1) * P],
                                     rhs=ident[:], is_transpose=True, start=False, stop=True,
                                 )
-                        nc.vector.tensor_reduce(
-                            out=y[:, 4 * q : 4 * q + 4, :, o],
-                            in_=bank[:].rearrange("p (s h l) -> p s h l", s=4, h=H, l=HALF),
-                            axis=AX.X,
-                            op=ALU.max,
-                        )
+                        for e in range(2):
+                            q = 2 * q2 + e
+                            nc.vector.tensor_reduce(
+                                out=y[:, 4 * q : 4 * q + 4, :, o],
+                                in_=banks[e][:].rearrange("p (s h l) -> p s h l", s=4, h=H, l=HALF),
+                                axis=AX.X,
+                                op=ALU.max,
+                            )
                 for t in range(TILES):
                     g = chunk * TILES + t
                     b, l0 = g // 2, (g % 2) * P

from contextlib import ExitStack

import concourse.mybir as mybir
from concourse.masks import make_identity

F32 = mybir.dt.float32
BF16 = mybir.dt.bfloat16
U32 = mybir.dt.uint32
U8 = mybir.dt.uint8
FP8X4 = mybir.dt.float8_e4m3fn_x4
ALU = mybir.AluOpType
ACT = mybir.ActivationFunctionType
AX = mybir.AxisListType

P = 128
B, L, D, H, DK = 16, 256, 512, 4, 64
E = H * DK
ROWS = B * L
HALF = DK // 2
CHUNK = 2048
TILES = CHUNK // P
PIECE = 512
CLAMP = 128.0

FLOPS = 2 * ROWS * D * 3 * E + 2 * 3 * ROWS * H * DK * DK


def tile_tropicalattention_pa_t_kernel(
    tc, x, Wq, Wk, Wv, lam, Wq_trop, Wk_trop, Wv_trop, out_0, out_1, out_2
):
    nc = tc.nc
    weights = [Wq, Wk, Wv]
    trops = [Wq_trop, Wk_trop, Wv_trop]
    outs = [out_0, out_1, out_2]

    with ExitStack() as ctx:
        const = ctx.enter_context(tc.tile_pool(name="const", bufs=1))
        keep = ctx.enter_context(tc.tile_pool(name="keep", bufs=1))
        tmp = ctx.enter_context(tc.tile_pool(name="tmp", bufs=3))
        psum = ctx.enter_context(tc.psum_pool(name="psum", bufs=8))

        ident = const.tile([P, P], F32, name="ident")
        make_identity(nc, ident[:])

        x_codes = keep.tile([P, ROWS], U32, name="x_codes", align_bytes=64)
        x_scales = keep.tile([P, ROWS], U8, name="x_scales", align_bytes=64)
        w_codes = [keep.tile([P, 2 * P], U32, name="w_codes%d" % j, align_bytes=64) for j in range(3)]
        w_scales = [keep.tile([P, 2 * P], U8, name="w_scales%d" % j, align_bytes=64) for j in range(3)]
        diff = [keep.tile([P, ROWS], F32, name="diff%d" % j) for j in range(3)]
        base = [keep.tile([P, ROWS], F32, name="base%d" % j) for j in range(3)]
        delta = [keep.tile([P, DK], F32, name="delta%d" % j) for j in range(3)]
        shift = [keep.tile([P, DK], F32, name="shift%d" % j) for j in range(3)]

        with tc.tile_pool(name="stage", bufs=2) as stage, tc.tile_pool(name="small", bufs=1) as small:
            w_sb = []
            for j in range(3):
                w_t = small.tile([P, 2 * D], BF16, name="w_sb%d" % j)
                nc.sync.dma_start(
                    out=w_t[:].rearrange("p (g k) -> p g k", g=2),
                    in_=weights[j].rearrange("(g p) k -> p g k", p=P),
                )
                w_sb.append(w_t)
            lam_b = small.tile([P, E], BF16, name="lam_b")
            nc.scalar.dma_start(out=lam_b[:], in_=lam.rearrange("a b e -> (a b e)").partition_broadcast(P))
            t_sb = []
            for j in range(3):
                t_t = small.tile([P, DK], BF16, name="t_sb%d" % j)
                nc.scalar.dma_start(out=t_t[0:DK, :], in_=trops[j])
                nc.scalar.dma_start(out=t_t[DK:P, :], in_=trops[j])
                t_sb.append(t_t)

            for j in range(3):
                words = w_sb[j][:].bitcast(F32)
                bank = psum.tile([P, 512], F32, name="bank", tag="bank")
                for g in range(2):
                    for u in range(2):
                        nc.tensor.transpose(
                            bank[:, u * 256 + g * P : u * 256 + (g + 1) * P],
                            words[:, g * 256 + u * P : g * 256 + (u + 1) * P],
                            ident[:],
                        )
                gw = small.tile([P, 2 * D], BF16, name="gw%d" % j, align_bytes=64)
                src = bank[:].rearrange("p (u h i l) -> p i h l u", u=2, h=H, i=2, l=HALF)
                dst = gw[:].bitcast(F32).rearrange("p (i h l u) -> p i h l u", i=2, h=H, l=HALF, u=2)
                for i in range(2):
                    nc.vector.tensor_copy(out=dst[:, i], in_=src[:, i])
                nc.vector.quantize_mx(out=w_codes[j][:].bitcast(FP8X4), scales=w_scales[j][:], in_=gw[:])

            lam_v = lam_b[:].rearrange("p (h i l) -> p h i l", h=H, i=2, l=HALF)
            for j in range(3):
                xab = small.tile([P, 2 * P], F32, name="xab%d" % j)
                for i in range(2):
                    nc.vector.tensor_tensor(
                        out=xab[:, i * P : (i + 1) * P].rearrange("p (h l) -> p h l", h=H),
                        in0=t_sb[j][:, i * HALF : (i + 1) * HALF].unsqueeze(1).to_broadcast([P, H, HALF]),
                        in1=lam_v[:, :, i, :],
                        op=ALU.subtract,
                    )
                bank = psum.tile([P, 512], F32, name="bank", tag="bank")
                for i in range(2):
                    nc.tensor.transpose(bank[:, i * P : (i + 1) * P], xab[:, i * P : (i + 1) * P], ident[:])
                tab = small.tile([P, 2, DK], F32, name="tab%d" % j)
                nc.vector.tensor_copy(
                    out=tab[:], in_=bank[:, 0 : 2 * P].rearrange("p (i o) -> p i o", i=2)[:, :, 0:DK]
                )
                nc.vector.tensor_tensor(out=delta[j][:], in0=tab[:, 0, :], in1=tab[:, 1, :], op=ALU.subtract)
                nc.vector.tensor_scalar(
                    out=delta[j][:], in0=delta[j][:], scalar1=CLAMP, scalar2=-CLAMP, op0=ALU.min, op1=ALU.max
                )
                nc.vector.scalar_tensor_tensor(
                    out=shift[j][:], in0=tab[:, 0, :], scalar=-CLAMP, in1=tab[:, 1, :], op0=ALU.add, op1=ALU.max
                )

            x_view = x.flatten_outer_dims().rearrange("(t p) k -> p t k", p=P)
            for c in range(4):
                xs = stage.tile([P, 8 * D], BF16, name="xs", tag="xs")
                nc.sync.dma_start(
                    out=xs[:].rearrange("p (t k) -> p t k", t=8), in_=x_view[:, 8 * c : 8 * c + 8, :]
                )
                words = xs[:].bitcast(F32)
                gx = stage.tile([P, 8 * D], BF16, name="gx", tag="gx", align_bytes=64)
                gx_words = gx[:].bitcast(F32)
                for pr in range(4):
                    bank = psum.tile([P, 512], F32, name="bank", tag="bank")
                    for tt in range(2):
                        for u in range(2):
                            t = 2 * pr + tt
                            nc.tensor.transpose(
                                bank[:, u * 256 + tt * P : u * 256 + (tt + 1) * P],
                                words[:, t * 256 + u * P : t * 256 + (u + 1) * P],
                                ident[:],
                            )
                    dst = gx_words[:, pr * 512 : (pr + 1) * 512].rearrange("p (r u) -> p r u", u=2)
                    src = bank[:].rearrange("p (u r) -> p r u", u=2)
                    if pr % 2 == 0:
                        nc.vector.tensor_copy(out=dst, in_=src)
                    else:
                        nc.scalar.copy(out=dst, in_=src)
                nc.vector.quantize_mx(
                    out=x_codes[:, c * 1024 : (c + 1) * 1024].bitcast(FP8X4),
                    scales=x_scales[:, c * 1024 : (c + 1) * 1024],
                    in_=gx[:],
                )

        relu_pool = ctx.enter_context(tc.tile_pool(name="relu_pool", bufs=3))
        base_pool = ctx.enter_context(tc.tile_pool(name="base_pool", bufs=3))
        y_pool = ctx.enter_context(tc.tile_pool(name="y_pool", bufs=2))

        def prep_piece(j, c):
            cols = slice(c * PIECE, (c + 1) * PIECE)
            for i in range(2):
                bank = psum.tile([P, 512], F32, name="bank", tag="bank")
                nc.tensor.matmul_mx(
                    out=bank[:],
                    lhsT=w_codes[j][:, i * P : (i + 1) * P].bitcast(FP8X4),
                    lhsT_scale=w_scales[j][:, i * P : (i + 1) * P],
                    rhs=x_codes[:, cols].bitcast(FP8X4),
                    rhs_scale=x_scales[:, cols],
                    start=True,
                    stop=True,
                )
                one_plus = tmp.tile([P, PIECE], F32, name="one_plus", tag="one_plus")
                nc.vector.tensor_scalar(
                    out=one_plus[:], in0=bank[:], scalar1=0.0, scalar2=1.0, op0=ALU.max, op1=ALU.add
                )
                target = diff[j] if i == 0 else base[j]
                nc.scalar.activation(out=target[:, cols], in_=one_plus[:], func=ACT.Ln)
            nc.vector.tensor_tensor(out=diff[j][:, cols], in0=diff[j][:, cols], in1=base[j][:, cols], op=ALU.subtract)

        pieces = [(j, c) for j in range(3) for c in range(ROWS // PIECE)]
        for k in range(4):
            prep_piece(*pieces[k])
        next_piece = 4

        step = 0
        for j in range(3):
            for chunk in range(ROWS // CHUNK):
                rows = slice(chunk * CHUNK, (chunk + 1) * CHUNK)
                y = y_pool.tile([P, TILES, H, DK], F32, name="y", tag="y")
                for o in range(DK):
                    if step % 16 == 0 and next_piece < len(pieces):
                        prep_piece(*pieces[next_piece])
                        next_piece += 1
                    step += 1
                    gain = relu_pool.tile([P, CHUNK], F32, name="gain", tag="gain")
                    nc.scalar.activation(
                        out=gain[:], in_=diff[j][:, rows], func=ACT.Relu, bias=delta[j][:, o : o + 1], scale=1.0
                    )
                    floor = base_pool.tile([P, CHUNK], F32, name="floor", tag="floor")
                    nc.gpsimd.tensor_scalar(
                        out=floor[:], in0=base[j][:, rows], scalar1=shift[j][:, o : o + 1], scalar2=1.0,
                        op0=ALU.add, op1=ALU.mult,
                    )
                    for q2 in range(TILES // 8):
                        banks = [psum.tile([P, 512], F32, name="bank", tag="bank") for e in range(2)]
                        for s in range(4):
                            for e in range(2):
                                t = 4 * (2 * q2 + e) + s
                                nc.tensor.matmul(
                                    out=banks[e][:, s * P : (s + 1) * P], lhsT=gain[:, t * P : (t + 1) * P],
                                    rhs=ident[:], is_transpose=True, start=True, stop=False,
                                )
                            for e in range(2):
                                t = 4 * (2 * q2 + e) + s
                                nc.tensor.matmul(
                                    out=banks[e][:, s * P : (s + 1) * P], lhsT=floor[:, t * P : (t + 1) * P],
                                    rhs=ident[:], is_transpose=True, start=False, stop=True,
                                )
                        for e in range(2):
                            q = 2 * q2 + e
                            nc.vector.tensor_reduce(
                                out=y[:, 4 * q : 4 * q + 4, :, o],
                                in_=banks[e][:].rearrange("p (s h l) -> p s h l", s=4, h=H, l=HALF),
                                axis=AX.X,
                                op=ALU.max,
                            )
                for t in range(TILES):
                    g = chunk * TILES + t
                    b, l0 = g // 2, (g % 2) * P
                    nc.sync.dma_start(
                        out=outs[j][b * H : (b + 1) * H, l0 : l0 + P, :].rearrange("h p o -> p h o"),
                        in_=y[:, t, :, :],
                    )
